import numpy as np
import ml_dtypes


def mxq(x, axis, fmt="e4m3"):
    dtype, down = {"e4m3": (ml_dtypes.float8_e4m3fn, 7), "e5m2": (ml_dtypes.float8_e5m2, 14)}[fmt]
    v = np.moveaxis(np.asarray(x, np.float32).astype(ml_dtypes.bfloat16).astype(np.float64), axis, -1)
    blocks = v.reshape(v.shape[:-1] + (-1, 32))
    amax = np.abs(blocks).max(-1, keepdims=True)
    byte = np.maximum(np.where(amax > 0, np.frexp(amax)[1] - 1 + 127, 0) - down, 1)
    scale = np.exp2(byte - 127.0)
    codes = (blocks / scale).astype(np.float32).astype(dtype).astype(np.float64)
    return np.moveaxis((codes * scale).reshape(v.shape), -1, axis)


WIDE = False


def mx_kscale(k):
    if not WIDE:
        return np.ones(k)
    levels = np.array([10, -10, 5, -5, 0])
    if k % 512:
        return np.exp2(np.random.permutation(np.resize(levels, k // 32))).repeat(32)
    a = np.empty((k // 512, 16))
    for p in range(k // 512):
        a[p, :8] = np.random.permutation(np.resize(levels, 8))
        for g in range(8):
            far = levels[np.abs(levels - a[p, g]) >= 10]
            a[p, g + 8] = far[np.random.randint(len(far))]
    return np.exp2(a.ravel()).repeat(32)


BF16 = ml_dtypes.bfloat16


def bf(x):
    return np.asarray(x, np.float32).astype(BF16)


def f64(x):
    return np.asarray(x).astype(np.float64)


B, N, D, H, DK, P = 4, 2048, 512, 2, 128, 512
E = H * DK


def setup_inputs():
    s = mx_kscale(D)
    return {"Q": bf(np.random.standard_normal((B, N, D)) * s),
            "WQ": bf(np.random.standard_normal((E, D)) * 1.5 / np.sqrt(D) / s)}


def core(Q, WQ):
    q = mxq(f64(Q), 2, "e4m3") @ mxq(f64(WQ), 1, "e4m3").T
    q = q.reshape(B, N, H, DK).transpose(0, 2, 1, 3)
    g = np.exp(q - q.max(-1, keepdims=True))
    return g / g.sum(-1, keepdims=True)


def e4m3fn_bytes(y):
    return np.clip(np.asarray(y, np.float64), -448.0, 448.0).astype(np.float32).astype(ml_dtypes.float8_e4m3fn).view(np.uint8)


def reference(Q, WQ):
    out = core(Q, WQ)
    s = np.max(np.abs(out)) / 448.0
    return out, e4m3fn_bytes(out / s)

@@ -1,0 +1,182 @@
+from contextlib import ExitStack
+
+import concourse.mybir as mybir
+from concourse.masks import make_identity
+
+B, N, D, H, DK = 4, 2048, 512, 2, 128
+FLOPS = 2 * B * N * D * H * DK
+
+F32 = mybir.dt.float32
+BF16 = mybir.dt.bfloat16
+U32 = mybir.dt.uint32
+U8 = mybir.dt.uint8
+FP8X4 = mybir.dt.float8_e4m3fn_x4
+FP8 = mybir.dt.float8_e4m3fn
+ACT = mybir.ActivationFunctionType
+ALU = mybir.AluOpType
+AX = mybir.AxisListType
+
+P = 128
+J = N // P
+GT = 4
+NG = B * J // GT
+VSPLIT = 1344
+
+
+def tile_multiheadattention_pb_t_kernel(tc, Q, WQ, out_0, out_1):
+    nc = tc.nc
+    q_view = Q.rearrange("b (p j) k -> b p j k", j=J)
+    w_view = WQ.rearrange("(h p) k -> p h k", p=P)
+    o0_view = out_0.rearrange("b h (p j) d -> b h p (j d)", j=J)
+    o1_view = out_1.rearrange("b h (p j) d -> b h p (j d)", j=J)
+
+    with ExitStack() as ctx:
+        ctx.enter_context(tc.manual_schedule())
+        const = ctx.enter_context(tc.tile_pool(name="const", bufs=1))
+        raw = ctx.enter_context(tc.tile_pool(name="raw", bufs=NG))
+        work = ctx.enter_context(tc.tile_pool(name="work", bufs=3))
+        keep = ctx.enter_context(tc.tile_pool(name="keep", bufs=1))
+        tps = ctx.enter_context(tc.psum_pool(name="tps", bufs=4))
+        qps = ctx.enter_context(tc.psum_pool(name="qps", bufs=4))
+
+        zero = const.tile([P, 1], F32, name="zero")
+        warm = const.tile([P, 1], F32, name="warm")
+        ident = const.tile([P, P], F32, name="ident")
+        sums = const.tile([P, 8 * NG + 1], F32, name="sums")
+        pmin = const.tile([P, 1], F32, name="pmin")
+        gmin = const.tile([P, 1], F32, name="gmin")
+        rfac = const.tile([P, 1], F32, name="rfac")
+        wraw = const.tile([P, H, D], BF16, name="wraw")
+        wgrp = const.tile([P, H * DK, 4], BF16, name="wgrp", align_bytes=64)
+        wcodes = const.tile([P, H * DK], U32, name="wcodes", align_bytes=64)
+        wscl = const.tile([P, H * DK], U8, name="wscl", align_bytes=64)
+        o0 = [[keep.tile([P, J * DK], F32, name="o0_%d_%d" % (b, h)) for h in range(H)] for b in range(B)]
+        f8 = [[keep.tile([P, J * DK], FP8, name="f8_%d_%d" % (b, h)) for h in range(H)] for b in range(B)]
+
+        nc.vector.memset(zero[:], 0.0)
+        nc.scalar.activation(out=warm[:], in_=zero[:], func=ACT.Exp)
+        make_identity(nc, ident[:])
+
+        qraw, xts, grps, cods, scls, qbs, nms, gts = {}, {}, {}, {}, {}, {}, {}, {}
+
+        def load(g):
+            b, j0 = g // GT, (g % GT) * GT
+            t = raw.tile([P, GT, D], BF16, name="qraw", tag="qraw")
+            qraw[g] = t
+            if g == 0:
+                nc.sync.dma_start(out=t[:, 0:2, :], in_=q_view[b, :, j0:j0 + 2, :])
+                nc.sync.dma_start(out=t[:, 2:4, :], in_=q_view[b, :, j0 + 2:j0 + 4, :])
+            else:
+                nc.sync.dma_start(out=t[:], in_=q_view[b, :, j0:j0 + GT, :])
+
+        def turn(g):
+            xts[g] = []
+            for half in range(2):
+                xt = tps.tile([P, 2, 2 * P], F32, name="xt", tag="xt")
+                xts[g].append(xt)
+                for a in range(2):
+                    words = qraw[g][:, 2 * half + a, :].bitcast(F32)
+                    for u in range(2):
+                        nc.tensor.transpose(out=xt[:, u, a * P:(a + 1) * P], in_=words[:, u:D // 2:2], identity=ident[:])
+
+        def copy_out(g):
+            grp = work.tile([P, GT * P, 4], BF16, name="grp", tag="grp", align_bytes=64)
+            grps[g] = grp
+            for half in range(2):
+                nc.scalar.copy(out=grp[:, half * 2 * P:(half + 1) * 2 * P, :].bitcast(F32),
+                               in_=xts[g][half][:].rearrange("p u r -> p r u"))
+
+        def quant(g):
+            cod = work.tile([P, GT * P], U32, name="cod", tag="cod", align_bytes=64)
+            scl = work.tile([P, GT * P], U8, name="scl", tag="scl", align_bytes=64)
+            cods[g], scls[g] = cod, scl
+            nc.vector.quantize_mx(out=cod[:].bitcast(FP8X4), scales=scl[:],
+                                  in_=grps[g][:].rearrange("p r t -> p (r t)"))
+
+        def mult(g):
+            qbs[g] = []
+            for half in range(2):
+                qb = qps.tile([P, 2, H * DK], F32, name="qb", tag="qb")
+                qbs[g].append(qb)
+                for a in range(2):
+                    cols = slice((2 * half + a) * P, (2 * half + a + 1) * P)
+                    nc.tensor.matmul_mx(out=qb[:, a, :], lhsT=cods[g][:, cols].bitcast(FP8X4), lhsT_scale=scls[g][:, cols],
+                                        rhs=wcodes[:].bitcast(FP8X4), rhs_scale=wscl[:], start=True, stop=True)
+
+        def rowmax(g):
+            nm = work.tile([P, 2 * GT], F32, name="nm", tag="nm")
+            nms[g] = nm
+            for half in range(2):
+                nc.vector.tensor_reduce(out=nm[:, 4 * half:4 * half + 4],
+                                        in_=qbs[g][half][:].rearrange("p a (h d) -> p (a h) d", h=H),
+                                        axis=AX.X, op=ALU.max, negate=True)
+
+        def expo(g):
+            gt = work.tile([P, 2 * GT, DK], F32, name="gt", tag="gt")
+            gts[g] = gt
+            for half in range(2):
+                for a in range(2):
+                    for h in range(H):
+                        c = 4 * half + 2 * a + h
+                        nc.scalar.activation(out=gt[:, c, :], in_=qbs[g][half][:, a, h * DK:(h + 1) * DK], func=ACT.Exp,
+                                             bias=nms[g][:, c:c + 1], scale=1.0,
+                                             accum_out=sums[:, 8 * g + c:8 * g + c + 1])
+
+        def norm(g):
+            b, j0 = g // GT, (g % GT) * GT
+            rs = work.tile([P, 2 * GT], F32, name="rs", tag="rs")
+            nc.vector.reciprocal(out=rs[:], in_=sums[:, 8 * g:8 * g + 8])
+            for h in range(H):
+                for t in range(GT):
+                    c = 2 * t + h
+                    nc.vector.tensor_scalar(out=o0[b][h][:, (j0 + t) * DK:(j0 + t + 1) * DK], in0=gts[g][:, c, :],
+                                            scalar1=rs[:, c:c + 1], scalar2=None, op0=ALU.mult)
+                cols = slice(j0 * DK, (j0 + GT) * DK)
+                nc.sync.dma_start(out=o0_view[b, h, :, cols], in_=o0[b][h][:, cols])
+
+        load(0)
+        nc.sync.dma_start(out=wraw[:], in_=w_view)
+        for g in range(1, NG):
+            load(g)
+
+        for i in range(NG + 2):
+            if i < NG:
+                turn(i)
+            if i == 0:
+                wt = tps.tile([P, 2, 2 * P], F32, name="xt", tag="xt")
+                for h in range(H):
+                    wwords = wraw[:, h, :].bitcast(F32)
+                    for u in range(2):
+                        nc.tensor.transpose(out=wt[:, u, h * P:(h + 1) * P], in_=wwords[:, u:D // 2:2], identity=ident[:])
+                nc.vector.tensor_copy(out=wgrp[:].bitcast(F32), in_=wt[:].rearrange("p u r -> p r u"))
+            if i == 1:
+                nc.vector.quantize_mx(out=wcodes[:].bitcast(FP8X4), scales=wscl[:],
+                                      in_=wgrp[:].rearrange("p r t -> p (r t)"))
+            if 1 <= i <= NG:
+                quant(i - 1)
+                mult(i - 1)
+            if i == NG + 1:
+                nc.vector.tensor_reduce(out=sums[:, 8 * NG:8 * NG + 1], in_=sums[:, 0:8 * (NG - 1)], axis=AX.X, op=ALU.min)
+            if 2 <= i:
+                expo(i - 2)
+            if i < NG:
+                copy_out(i)
+            if 3 <= i:
+                norm(i - 3)
+            if 1 <= i <= NG:
+                rowmax(i - 1)
+
+        nc.vector.tensor_reduce(out=pmin[:], in_=sums[:, 8 * (NG - 1):8 * NG + 1], axis=AX.X, op=ALU.min)
+        at = tps.tile([P, 2, 2 * P], F32, name="xt", tag="xt")
+        nc.tensor.transpose(out=at[:, 0, 0:P], in_=pmin[:, 0:1].to_broadcast([P, P]), identity=ident[:])
+        norm(NG - 1)
+        nc.vector.tensor_reduce(out=gmin[:], in_=at[:, 0, 0:P], axis=AX.X, op=ALU.min)
+        nc.vector.tensor_scalar(out=rfac[:], in0=gmin[:], scalar1=448.0, scalar2=None, op0=ALU.mult)
+
+        for b in range(B):
+            for h in range(H):
+                nc.vector.tensor_scalar(out=f8[b][h][:, 0:VSPLIT], in0=o0[b][h][:, 0:VSPLIT], scalar1=rfac[:, 0:1],
+                                        scalar2=None, op0=ALU.mult, saturate=False)
+                nc.scalar.activation(out=f8[b][h][:, VSPLIT:J * DK], in_=o0[b][h][:, VSPLIT:J * DK], func=ACT.Identity,
+                                     scale=rfac[:, 0:1], bias=zero[:, 0:1], saturate=False)
+                nc.sync.dma_start(out=o1_view[b, h], in_=f8[b][h][:].bitcast(U8))

@@ -21,6 +21,9 @@ J = N // P
 GT = 4
 NG = B * J // GT
 VSPLIT = 1344
+VFIRST = 1
+VCOPY = [0, 1]
+GHEADS = []
 
 
 def tile_multiheadattention_pb_t_kernel(tc, Q, WQ, out_0, out_1):
@@ -34,7 +37,7 @@ def tile_multiheadattention_pb_t_kernel(tc, Q, WQ, out_0, out_1):
         ctx.enter_context(tc.manual_schedule())
         const = ctx.enter_context(tc.tile_pool(name="const", bufs=1))
         raw = ctx.enter_context(tc.tile_pool(name="raw", bufs=NG))
-        work = ctx.enter_context(tc.tile_pool(name="work", bufs=3))
+        work = ctx.enter_context(tc.tile_pool(name="work", bufs=4))
         keep = ctx.enter_context(tc.tile_pool(name="keep", bufs=1))
         tps = ctx.enter_context(tc.psum_pool(name="tps", bufs=4))
         qps = ctx.enter_context(tc.psum_pool(name="qps", bufs=4))
@@ -57,7 +60,7 @@ def tile_multiheadattention_pb_t_kernel(tc, Q, WQ, out_0, out_1):
         nc.scalar.activation(out=warm[:], in_=zero[:], func=ACT.Exp)
         make_identity(nc, ident[:])
 
-        qraw, xts, grps, cods, scls, qbs, nms, gts = {}, {}, {}, {}, {}, {}, {}, {}
+        qraw, xts, grps, cods, scls, qbs, nms, gts, rss = {}, {}, {}, {}, {}, {}, {}, {}, {}
 
         def load(g):
             b, j0 = g // GT, (g % GT) * GT
@@ -79,12 +82,16 @@ def tile_multiheadattention_pb_t_kernel(tc, Q, WQ, out_0, out_1):
                     for u in range(2):
                         nc.tensor.transpose(out=xt[:, u, a * P:(a + 1) * P], in_=words[:, u:D // 2:2], identity=ident[:])
 
-        def copy_out(g):
-            grp = work.tile([P, GT * P, 4], BF16, name="grp", tag="grp", align_bytes=64)
-            grps[g] = grp
-            for half in range(2):
-                nc.scalar.copy(out=grp[:, half * 2 * P:(half + 1) * 2 * P, :].bitcast(F32),
-                               in_=xts[g][half][:].rearrange("p u r -> p r u"))
+        def new_grp(g):
+            grps[g] = work.tile([P, GT * P, 4], BF16, name="grp", tag="grp", align_bytes=64)
+
+        def copy_out(g, half, on_vector):
+            dst = grps[g][:, half * 2 * P:(half + 1) * 2 * P, :].bitcast(F32)
+            src = xts[g][half][:].rearrange("p u r -> p r u")
+            if on_vector:
+                nc.vector.tensor_copy(out=dst, in_=src)
+            else:
+                nc.scalar.copy(out=dst, in_=src)
 
         def quant(g):
             cod = work.tile([P, GT * P], U32, name="cod", tag="cod", align_bytes=64)
@@ -100,8 +107,9 @@ def tile_multiheadattention_pb_t_kernel(tc, Q, WQ, out_0, out_1):
                 qbs[g].append(qb)
                 for a in range(2):
                     cols = slice((2 * half + a) * P, (2 * half + a + 1) * P)
-                    nc.tensor.matmul_mx(out=qb[:, a, :], lhsT=cods[g][:, cols].bitcast(FP8X4), lhsT_scale=scls[g][:, cols],
-                                        rhs=wcodes[:].bitcast(FP8X4), rhs_scale=wscl[:], start=True, stop=True)
+                    for rep in range(2):
+                        nc.tensor.matmul_mx(out=qb[:, a, :], lhsT=cods[g][:, cols].bitcast(FP8X4), lhsT_scale=scls[g][:, cols],
+                                            rhs=wcodes[:].bitcast(FP8X4), rhs_scale=wscl[:], start=True, stop=True)
 
         def rowmax(g):
             nm = work.tile([P, 2 * GT], F32, name="nm", tag="nm")
@@ -122,15 +130,25 @@ def tile_multiheadattention_pb_t_kernel(tc, Q, WQ, out_0, out_1):
                                              bias=nms[g][:, c:c + 1], scale=1.0,
                                              accum_out=sums[:, 8 * g + c:8 * g + c + 1])
 
-        def norm(g):
-            b, j0 = g // GT, (g % GT) * GT
+        def recip(g):
             rs = work.tile([P, 2 * GT], F32, name="rs", tag="rs")
+            rss[g] = rs
             nc.vector.reciprocal(out=rs[:], in_=sums[:, 8 * g:8 * g + 8])
+
+        def norm(g, engs):
+            b, j0 = g // GT, (g % GT) * GT
+            rs = rss[g]
             for h in range(H):
                 for t in range(GT):
                     c = 2 * t + h
-                    nc.vector.tensor_scalar(out=o0[b][h][:, (j0 + t) * DK:(j0 + t + 1) * DK], in0=gts[g][:, c, :],
-                                            scalar1=rs[:, c:c + 1], scalar2=None, op0=ALU.mult)
+                    dst = o0[b][h][:, (j0 + t) * DK:(j0 + t + 1) * DK]
+                    if engs[h] == "v":
+                        nc.vector.tensor_scalar(out=dst, in0=gts[g][:, c, :], scalar1=rs[:, c:c + 1], scalar2=None, op0=ALU.mult)
+                    elif engs[h] == "g":
+                        nc.gpsimd.tensor_scalar(out=dst, in0=gts[g][:, c, :], scalar1=rs[:, c:c + 1], scalar2=0.0,
+                                                op0=ALU.mult, op1=ALU.add)
+                    else:
+                        nc.scalar.activation(out=dst, in_=gts[g][:, c, :], func=ACT.Copy, scale=rs[:, c:c + 1])
                 cols = slice(j0 * DK, (j0 + GT) * DK)
                 nc.sync.dma_start(out=o0_view[b, h, :, cols], in_=o0[b][h][:, cols])
 
@@ -139,9 +157,11 @@ def tile_multiheadattention_pb_t_kernel(tc, Q, WQ, out_0, out_1):
         for g in range(1, NG):
             load(g)
 
-        for i in range(NG + 2):
+        steady = ["g" if h in GHEADS else "v" for h in range(H)]
+        for i in range(NG + 3):
             if i < NG:
                 turn(i)
+                new_grp(i)
             if i == 0:
                 wt = tps.tile([P, 2, 2 * P], F32, name="xt", tag="xt")
                 for h in range(H):
@@ -152,31 +172,40 @@ def tile_multiheadattention_pb_t_kernel(tc, Q, WQ, out_0, out_1):
             if i == 1:
                 nc.vector.quantize_mx(out=wcodes[:].bitcast(FP8X4), scales=wscl[:],
                                       in_=wgrp[:].rearrange("p r t -> p (r t)"))
+            if 4 <= i:
+                recip(i - 4)
             if 1 <= i <= NG:
                 quant(i - 1)
-                mult(i - 1)
-            if i == NG + 1:
+            if 2 <= i <= NG + 1:
+                mult(i - 2)
+            if i == NG + 2:
                 nc.vector.tensor_reduce(out=sums[:, 8 * NG:8 * NG + 1], in_=sums[:, 0:8 * (NG - 1)], axis=AX.X, op=ALU.min)
-            if 2 <= i:
-                expo(i - 2)
-            if i < NG:
-                copy_out(i)
+            if 4 <= i:
+                norm(i - 4, steady)
             if 3 <= i:
-                norm(i - 3)
-            if 1 <= i <= NG:
-                rowmax(i - 1)
+                expo(i - 3)
+            if i < NG:
+                copy_out(i, 0, i in VCOPY)
+                copy_out(i, 1, False)
+            if 2 <= i <= NG + 1:
+                rowmax(i - 2)
 
         nc.vector.tensor_reduce(out=pmin[:], in_=sums[:, 8 * (NG - 1):8 * NG + 1], axis=AX.X, op=ALU.min)
         at = tps.tile([P, 2, 2 * P], F32, name="xt", tag="xt")
         nc.tensor.transpose(out=at[:, 0, 0:P], in_=pmin[:, 0:1].to_broadcast([P, P]), identity=ident[:])
-        norm(NG - 1)
+        recip(NG - 1)
+        norm(NG - 1, ["s", "s"])
         nc.vector.tensor_reduce(out=gmin[:], in_=at[:, 0, 0:P], axis=AX.X, op=ALU.min)
         nc.vector.tensor_scalar(out=rfac[:], in0=gmin[:], scalar1=448.0, scalar2=None, op0=ALU.mult)
 
+        n = 0
         for b in range(B):
             for h in range(H):
-                nc.vector.tensor_scalar(out=f8[b][h][:, 0:VSPLIT], in0=o0[b][h][:, 0:VSPLIT], scalar1=rfac[:, 0:1],
+                vs = J * DK if n < VFIRST else VSPLIT
+                n += 1
+                nc.vector.tensor_scalar(out=f8[b][h][:, 0:vs], in0=o0[b][h][:, 0:vs], scalar1=rfac[:, 0:1],
                                         scalar2=None, op0=ALU.mult, saturate=False)
-                nc.scalar.activation(out=f8[b][h][:, VSPLIT:J * DK], in_=o0[b][h][:, VSPLIT:J * DK], func=ACT.Identity,
-                                     scale=rfac[:, 0:1], bias=zero[:, 0:1], saturate=False)
+                if vs < J * DK:
+                    nc.scalar.activation(out=f8[b][h][:, vs:J * DK], in_=o0[b][h][:, vs:J * DK], func=ACT.Identity,
+                                         scale=rfac[:, 0:1], bias=zero[:, 0:1], saturate=False)
                 nc.sync.dma_start(out=o1_view[b, h], in_=f8[b][h][:].bitcast(U8))

@@ -18,16 +18,20 @@ AX = mybir.AxisListType
 
 P = 128
 J = N // P
-GT = 4
-NG = B * J // GT
-VSPLIT = 1344
+NPAIR = B * J // 2
+PPB = J // 2
+SIZES = [1, 1] + [2] * 15
+NG = 17
+VCOPY = [2, 3, 4, 5, 8, 11, 14]
+LAG_Q, LAG_X, LAG_E, LAG_N = 1, 2, 3, 5
+VSPLIT = 1280
 VFIRST = 1
-VCOPY = [0, 1]
-GHEADS = []
+LAST_ON_SCALAR = 4
 
 
 def tile_multiheadattention_pb_t_kernel(tc, Q, WQ, out_0, out_1):
     nc = tc.nc
+    FIRST = [sum(SIZES[:g]) for g in range(NG)]
     q_view = Q.rearrange("b (p j) k -> b p j k", j=J)
     w_view = WQ.rearrange("(h p) k -> p h k", p=P)
     o0_view = out_0.rearrange("b h (p j) d -> b h p (j d)", j=J)
@@ -37,7 +41,7 @@ def tile_multiheadattention_pb_t_kernel(tc, Q, WQ, out_0, out_1):
         ctx.enter_context(tc.manual_schedule())
         const = ctx.enter_context(tc.tile_pool(name="const", bufs=1))
         raw = ctx.enter_context(tc.tile_pool(name="raw", bufs=NG))
-        work = ctx.enter_context(tc.tile_pool(name="work", bufs=4))
+        work = ctx.enter_context(tc.tile_pool(name="work", bufs=5))
         keep = ctx.enter_context(tc.tile_pool(name="keep", bufs=1))
         tps = ctx.enter_context(tc.psum_pool(name="tps", bufs=4))
         qps = ctx.enter_context(tc.psum_pool(name="qps", bufs=4))
@@ -45,9 +49,9 @@ def tile_multiheadattention_pb_t_kernel(tc, Q, WQ, out_0, out_1):
         zero = const.tile([P, 1], F32, name="zero")
         warm = const.tile([P, 1], F32, name="warm")
         ident = const.tile([P, P], F32, name="ident")
-        sums = const.tile([P, 8 * NG + 1], F32, name="sums")
+        sums = const.tile([P, 4 * NPAIR + 1], F32, name="sums")
         pmin = const.tile([P, 1], F32, name="pmin")
-        gmin = const.tile([P, 1], F32, name="gmin")
+        scaled = const.tile([P, P], F32, name="scaled")
         rfac = const.tile([P, 1], F32, name="rfac")
         wraw = const.tile([P, H, D], BF16, name="wraw")
         wgrp = const.tile([P, H * DK, 4], BF16, name="wgrp", align_bytes=64)
@@ -62,94 +66,95 @@ def tile_multiheadattention_pb_t_kernel(tc, Q, WQ, out_0, out_1):
 
         qraw, xts, grps, cods, scls, qbs, nms, gts, rss = {}, {}, {}, {}, {}, {}, {}, {}, {}
 
+        def pairs(g):
+            return range(FIRST[g], FIRST[g] + SIZES[g])
+
         def load(g):
-            b, j0 = g // GT, (g % GT) * GT
-            t = raw.tile([P, GT, D], BF16, name="qraw", tag="qraw")
+            b, j0 = FIRST[g] // PPB, 2 * (FIRST[g] % PPB)
+            t = raw.tile([P, 2 * SIZES[g], D], BF16, name="qraw", tag="qraw")
             qraw[g] = t
-            if g == 0:
-                nc.sync.dma_start(out=t[:, 0:2, :], in_=q_view[b, :, j0:j0 + 2, :])
-                nc.sync.dma_start(out=t[:, 2:4, :], in_=q_view[b, :, j0 + 2:j0 + 4, :])
-            else:
-                nc.sync.dma_start(out=t[:], in_=q_view[b, :, j0:j0 + GT, :])
+            nc.sync.dma_start(out=t[:], in_=q_view[b, :, j0:j0 + 2 * SIZES[g], :])
 
         def turn(g):
-            xts[g] = []
-            for half in range(2):
+            for q in pairs(g):
                 xt = tps.tile([P, 2, 2 * P], F32, name="xt", tag="xt")
-                xts[g].append(xt)
+                xts[q] = xt
                 for a in range(2):
-                    words = qraw[g][:, 2 * half + a, :].bitcast(F32)
+                    words = qraw[g][:, 2 * (q - FIRST[g]) + a, :].bitcast(F32)
                     for u in range(2):
                         nc.tensor.transpose(out=xt[:, u, a * P:(a + 1) * P], in_=words[:, u:D // 2:2], identity=ident[:])
 
-        def new_grp(g):
-            grps[g] = work.tile([P, GT * P, 4], BF16, name="grp", tag="grp", align_bytes=64)
-
-        def copy_out(g, half, on_vector):
-            dst = grps[g][:, half * 2 * P:(half + 1) * 2 * P, :].bitcast(F32)
-            src = xts[g][half][:].rearrange("p u r -> p r u")
-            if on_vector:
-                nc.vector.tensor_copy(out=dst, in_=src)
-            else:
-                nc.scalar.copy(out=dst, in_=src)
+        def copy_out(g, on_vector):
+            if g not in grps:
+                grps[g] = work.tile([P, SIZES[g] * 2 * P, 4], BF16, name="grp", tag="grp", align_bytes=64)
+            for q in pairs(g):
+                v = g in VCOPY and q == FIRST[g] + SIZES[g] - 1
+                if v != on_vector:
+                    continue
+                l = q - FIRST[g]
+                dst = grps[g][:, l * 2 * P:(l + 1) * 2 * P, :].bitcast(F32)
+                src = xts[q][:].rearrange("p u r -> p r u")
+                if on_vector:
+                    nc.vector.tensor_copy(out=dst, in_=src)
+                else:
+                    nc.scalar.copy(out=dst, in_=src)
 
         def quant(g):
-            cod = work.tile([P, GT * P], U32, name="cod", tag="cod", align_bytes=64)
-            scl = work.tile([P, GT * P], U8, name="scl", tag="scl", align_bytes=64)
+            cod = work.tile([P, SIZES[g] * 2 * P], U32, name="cod", tag="cod", align_bytes=64)
+            scl = work.tile([P, SIZES[g] * 2 * P], U8, name="scl", tag="scl", align_bytes=64)
             cods[g], scls[g] = cod, scl
             nc.vector.quantize_mx(out=cod[:].bitcast(FP8X4), scales=scl[:],
                                   in_=grps[g][:].rearrange("p r t -> p (r t)"))
 
         def mult(g):
-            qbs[g] = []
-            for half in range(2):
+            for q in pairs(g):
                 qb = qps.tile([P, 2, H * DK], F32, name="qb", tag="qb")
-                qbs[g].append(qb)
+                qbs[q] = qb
                 for a in range(2):
-                    cols = slice((2 * half + a) * P, (2 * half + a + 1) * P)
-                    for rep in range(2):
-                        nc.tensor.matmul_mx(out=qb[:, a, :], lhsT=cods[g][:, cols].bitcast(FP8X4), lhsT_scale=scls[g][:, cols],
-                                            rhs=wcodes[:].bitcast(FP8X4), rhs_scale=wscl[:], start=True, stop=True)
+                    c0 = (2 * (q - FIRST[g]) + a) * P
+                    nc.tensor.matmul_mx(out=qb[:, a, :], lhsT=cods[g][:, c0:c0 + P].bitcast(FP8X4), lhsT_scale=scls[g][:, c0:c0 + P],
+                                        rhs=wcodes[:].bitcast(FP8X4), rhs_scale=wscl[:], start=True, stop=True)
 
         def rowmax(g):
-            nm = work.tile([P, 2 * GT], F32, name="nm", tag="nm")
+            nm = work.tile([P, 4 * SIZES[g]], F32, name="nm", tag="nm")
             nms[g] = nm
-            for half in range(2):
-                nc.vector.tensor_reduce(out=nm[:, 4 * half:4 * half + 4],
-                                        in_=qbs[g][half][:].rearrange("p a (h d) -> p (a h) d", h=H),
+            for q in pairs(g):
+                l = q - FIRST[g]
+                nc.vector.tensor_reduce(out=nm[:, 4 * l:4 * l + 4],
+                                        in_=qbs[q][:].rearrange("p a (h d) -> p (a h) d", h=H),
                                         axis=AX.X, op=ALU.max, negate=True)
 
         def expo(g):
-            gt = work.tile([P, 2 * GT, DK], F32, name="gt", tag="gt")
+            gt = work.tile([P, 4 * SIZES[g], DK], F32, name="gt", tag="gt")
             gts[g] = gt
-            for half in range(2):
+            for q in pairs(g):
+                l = q - FIRST[g]
                 for a in range(2):
                     for h in range(H):
-                        c = 4 * half + 2 * a + h
-                        nc.scalar.activation(out=gt[:, c, :], in_=qbs[g][half][:, a, h * DK:(h + 1) * DK], func=ACT.Exp,
+                        c = 4 * l + 2 * a + h
+                        nc.scalar.activation(out=gt[:, c, :], in_=qbs[q][:, a, h * DK:(h + 1) * DK], func=ACT.Exp,
                                              bias=nms[g][:, c:c + 1], scale=1.0,
-                                             accum_out=sums[:, 8 * g + c:8 * g + c + 1])
+                                             accum_out=sums[:, 4 * FIRST[g] + c:4 * FIRST[g] + c + 1])
 
         def recip(g):
-            rs = work.tile([P, 2 * GT], F32, name="rs", tag="rs")
+            rs = work.tile([P, 4 * SIZES[g]], F32, name="rs", tag="rs")
             rss[g] = rs
-            nc.vector.reciprocal(out=rs[:], in_=sums[:, 8 * g:8 * g + 8])
+            nc.vector.reciprocal(out=rs[:], in_=sums[:, 4 * FIRST[g]:4 * (FIRST[g] + SIZES[g])])
 
-        def norm(g, engs):
-            b, j0 = g // GT, (g % GT) * GT
+        def norm(g, on_scalar):
+            b, j0 = FIRST[g] // PPB, 2 * (FIRST[g] % PPB)
             rs = rss[g]
+            n = 0
             for h in range(H):
-                for t in range(GT):
+                for t in range(2 * SIZES[g]):
                     c = 2 * t + h
                     dst = o0[b][h][:, (j0 + t) * DK:(j0 + t + 1) * DK]
-                    if engs[h] == "v":
-                        nc.vector.tensor_scalar(out=dst, in0=gts[g][:, c, :], scalar1=rs[:, c:c + 1], scalar2=None, op0=ALU.mult)
-                    elif engs[h] == "g":
-                        nc.gpsimd.tensor_scalar(out=dst, in0=gts[g][:, c, :], scalar1=rs[:, c:c + 1], scalar2=0.0,
-                                                op0=ALU.mult, op1=ALU.add)
-                    else:
+                    n += 1
+                    if n > 4 * SIZES[g] - on_scalar:
                         nc.scalar.activation(out=dst, in_=gts[g][:, c, :], func=ACT.Copy, scale=rs[:, c:c + 1])
-                cols = slice(j0 * DK, (j0 + GT) * DK)
+                    else:
+                        nc.vector.tensor_scalar(out=dst, in0=gts[g][:, c, :], scalar1=rs[:, c:c + 1], scalar2=None, op0=ALU.mult)
+                cols = slice(j0 * DK, (j0 + 2 * SIZES[g]) * DK)
                 nc.sync.dma_start(out=o0_view[b, h, :, cols], in_=o0[b][h][:, cols])
 
         load(0)
@@ -157,46 +162,46 @@ def tile_multiheadattention_pb_t_kernel(tc, Q, WQ, out_0, out_1):
         for g in range(1, NG):
             load(g)
 
-        steady = ["g" if h in GHEADS else "v" for h in range(H)]
-        for i in range(NG + 3):
-            if i < NG:
-                turn(i)
-                new_grp(i)
-            if i == 0:
-                wt = tps.tile([P, 2, 2 * P], F32, name="xt", tag="xt")
-                for h in range(H):
-                    wwords = wraw[:, h, :].bitcast(F32)
-                    for u in range(2):
-                        nc.tensor.transpose(out=wt[:, u, h * P:(h + 1) * P], in_=wwords[:, u:D // 2:2], identity=ident[:])
-                nc.vector.tensor_copy(out=wgrp[:].bitcast(F32), in_=wt[:].rearrange("p u r -> p r u"))
-            if i == 1:
+        turn(0)
+        wt = tps.tile([P, 2, 2 * P], F32, name="xt", tag="xt")
+        for h in range(H):
+            wwords = wraw[:, h, :].bitcast(F32)
+            for u in range(2):
+                nc.tensor.transpose(out=wt[:, u, h * P:(h + 1) * P], in_=wwords[:, u:D // 2:2], identity=ident[:])
+        nc.vector.tensor_copy(out=wgrp[:].bitcast(F32), in_=wt[:].rearrange("p u r -> p r u"))
+
+        for s in range(NG + LAG_N - 1):
+            if 0 <= s - LAG_X < NG:
+                mult(s - LAG_X)
+            if s + 1 < NG:
+                turn(s + 1)
+            if s < NG:
+                copy_out(s, False)
+            if 0 <= s - LAG_E < NG:
+                expo(s - LAG_E)
+            if 0 <= s - LAG_N:
+                recip(s - LAG_N)
+            if s == 1:
                 nc.vector.quantize_mx(out=wcodes[:].bitcast(FP8X4), scales=wscl[:],
                                       in_=wgrp[:].rearrange("p r t -> p (r t)"))
-            if 4 <= i:
-                recip(i - 4)
-            if 1 <= i <= NG:
-                quant(i - 1)
-            if 2 <= i <= NG + 1:
-                mult(i - 2)
-            if i == NG + 2:
-                nc.vector.tensor_reduce(out=sums[:, 8 * NG:8 * NG + 1], in_=sums[:, 0:8 * (NG - 1)], axis=AX.X, op=ALU.min)
-            if 4 <= i:
-                norm(i - 4, steady)
-            if 3 <= i:
-                expo(i - 3)
-            if i < NG:
-                copy_out(i, 0, i in VCOPY)
-                copy_out(i, 1, False)
-            if 2 <= i <= NG + 1:
-                rowmax(i - 2)
+            if 0 <= s - LAG_Q < NG:
+                quant(s - LAG_Q)
+            if s < NG:
+                copy_out(s, True)
+            if 0 <= s - LAG_N:
+                norm(s - LAG_N, 0)
+            if 0 <= s - LAG_X < NG:
+                rowmax(s - LAG_X)
+            if s == NG + LAG_E - 1:
+                nc.vector.tensor_reduce(out=sums[:, 4 * NPAIR:4 * NPAIR + 1], in_=sums[:, 0:4 * FIRST[NG - 1]], axis=AX.X, op=ALU.min)
 
-        nc.vector.tensor_reduce(out=pmin[:], in_=sums[:, 8 * (NG - 1):8 * NG + 1], axis=AX.X, op=ALU.min)
+        nc.vector.tensor_reduce(out=pmin[:], in_=sums[:, 4 * FIRST[NG - 1]:4 * NPAIR + 1], axis=AX.X, op=ALU.min)
         at = tps.tile([P, 2, 2 * P], F32, name="xt", tag="xt")
         nc.tensor.transpose(out=at[:, 0, 0:P], in_=pmin[:, 0:1].to_broadcast([P, P]), identity=ident[:])
         recip(NG - 1)
-        norm(NG - 1, ["s", "s"])
-        nc.vector.tensor_reduce(out=gmin[:], in_=at[:, 0, 0:P], axis=AX.X, op=ALU.min)
-        nc.vector.tensor_scalar(out=rfac[:], in0=gmin[:], scalar1=448.0, scalar2=None, op0=ALU.mult)
+        norm(NG - 1, LAST_ON_SCALAR)
+        nc.vector.tensor_scalar(out=scaled[:], in0=at[:, 0, 0:P], scalar1=448.0, scalar2=None, op0=ALU.mult, op1=ALU.min,
+                                accum_out=rfac[:, 0:1])
 
         n = 0
         for b in range(B):
@@ -208,4 +213,8 @@ def tile_multiheadattention_pb_t_kernel(tc, Q, WQ, out_0, out_1):
                 if vs < J * DK:
                     nc.scalar.activation(out=f8[b][h][:, vs:J * DK], in_=o0[b][h][:, vs:J * DK], func=ACT.Identity,
                                          scale=rfac[:, 0:1], bias=zero[:, 0:1], saturate=False)
-                nc.sync.dma_start(out=o1_view[b, h], in_=f8[b][h][:].bitcast(U8))
+                if n < B * H:
+                    nc.sync.dma_start(out=o1_view[b, h], in_=f8[b][h][:].bitcast(U8))
+                else:
+                    nc.sync.dma_start(out=o1_view[b, h, :, 0:vs], in_=f8[b][h][:, 0:vs].bitcast(U8))
+                    nc.sync.dma_start(out=o1_view[b, h, :, vs:J * DK], in_=f8[b][h][:, vs:J * DK].bitcast(U8))

@@ -22,7 +22,7 @@ NPAIR = B * J // 2
 PPB = J // 2
 SIZES = [1, 1] + [2] * 15
 NG = 17
-VCOPY = [2, 3, 4, 5, 8, 11, 14]
+VCOPY = [2, 3, 4]
 LAG_Q, LAG_X, LAG_E, LAG_N = 1, 2, 3, 5
 VSPLIT = 1280
 VFIRST = 1

@@ -22,8 +22,9 @@ NPAIR = B * J // 2
 PPB = J // 2
 SIZES = [1, 1] + [2] * 15
 NG = 17
-VCOPY = [2, 3, 4]
-LAG_Q, LAG_X, LAG_E, LAG_N = 1, 2, 3, 5
+VCOPY = [2, 3, 4, 5, 10]
+LAG_Q, LAG_X, LAG_E, LAG_R, LAG_N = 1, 2, 3, 4, 5
+GUNITS = 2
 VSPLIT = 1280
 VFIRST = 1
 LAST_ON_SCALAR = 4
@@ -141,7 +142,13 @@ def tile_multiheadattention_pb_t_kernel(tc, Q, WQ, out_0, out_1):
             rss[g] = rs
             nc.vector.reciprocal(out=rs[:], in_=sums[:, 4 * FIRST[g]:4 * (FIRST[g] + SIZES[g])])
 
-        def norm(g, on_scalar):
+        def gnorm(g):
+            b, j0 = FIRST[g] // PPB, 2 * (FIRST[g] % PPB)
+            nc.gpsimd.tensor_tensor(out=o0[b][1][:, j0 * DK:(j0 + GUNITS) * DK].rearrange("p (t d) -> p t d", d=DK),
+                                    in0=gts[g][:, 1:2 * GUNITS:2, :],
+                                    in1=rss[g][:, 1:2 * GUNITS:2].unsqueeze(2).to_broadcast([P, GUNITS, DK]), op=ALU.mult)
+
+        def norm(g, on_scalar, skip):
             b, j0 = FIRST[g] // PPB, 2 * (FIRST[g] % PPB)
             rs = rss[g]
             n = 0
@@ -150,6 +157,8 @@ def tile_multiheadattention_pb_t_kernel(tc, Q, WQ, out_0, out_1):
                     c = 2 * t + h
                     dst = o0[b][h][:, (j0 + t) * DK:(j0 + t + 1) * DK]
                     n += 1
+                    if h == 1 and t < skip:
+                        continue
                     if n > 4 * SIZES[g] - on_scalar:
                         nc.scalar.activation(out=dst, in_=gts[g][:, c, :], func=ACT.Copy, scale=rs[:, c:c + 1])
                     else:
@@ -179,17 +188,19 @@ def tile_multiheadattention_pb_t_kernel(tc, Q, WQ, out_0, out_1):
                 copy_out(s, False)
             if 0 <= s - LAG_E < NG:
                 expo(s - LAG_E)
-            if 0 <= s - LAG_N:
-                recip(s - LAG_N)
             if s == 1:
                 nc.vector.quantize_mx(out=wcodes[:].bitcast(FP8X4), scales=wscl[:],
                                       in_=wgrp[:].rearrange("p r t -> p (r t)"))
             if 0 <= s - LAG_Q < NG:
                 quant(s - LAG_Q)
+            if 0 <= s - LAG_N:
+                norm(s - LAG_N, 0, GUNITS if SIZES[s - LAG_N] == 2 else 0)
+            if 0 <= s - LAG_R < NG - 1:
+                recip(s - LAG_R)
+                if SIZES[s - LAG_R] == 2:
+                    gnorm(s - LAG_R)
             if s < NG:
                 copy_out(s, True)
-            if 0 <= s - LAG_N:
-                norm(s - LAG_N, 0)
             if 0 <= s - LAG_X < NG:
                 rowmax(s - LAG_X)
             if s == NG + LAG_E - 1:
@@ -199,7 +210,7 @@ def tile_multiheadattention_pb_t_kernel(tc, Q, WQ, out_0, out_1):
         at = tps.tile([P, 2, 2 * P], F32, name="xt", tag="xt")
         nc.tensor.transpose(out=at[:, 0, 0:P], in_=pmin[:, 0:1].to_broadcast([P, P]), identity=ident[:])
         recip(NG - 1)
-        norm(NG - 1, LAST_ON_SCALAR)
+        norm(NG - 1, LAST_ON_SCALAR, 0)
         nc.vector.tensor_scalar(out=scaled[:], in0=at[:, 0, 0:P], scalar1=448.0, scalar2=None, op0=ALU.mult, op1=ALU.min,
                                 accum_out=rfac[:, 0:1])
 

@@ -22,7 +22,7 @@ NPAIR = B * J // 2
 PPB = J // 2
 SIZES = [1, 1] + [2] * 15
 NG = 17
-VCOPY = [2, 3, 4, 5, 10]
+VCOPY = [2, 3, 4, 5]
 LAG_Q, LAG_X, LAG_E, LAG_R, LAG_N = 1, 2, 3, 4, 5
 GUNITS = 2
 VSPLIT = 1280
@@ -194,10 +194,10 @@ def tile_multiheadattention_pb_t_kernel(tc, Q, WQ, out_0, out_1):
             if 0 <= s - LAG_Q < NG:
                 quant(s - LAG_Q)
             if 0 <= s - LAG_N:
-                norm(s - LAG_N, 0, GUNITS if SIZES[s - LAG_N] == 2 else 0)
+                norm(s - LAG_N, 0, GUNITS if 2 <= s - LAG_N < NG - 2 else 0)
             if 0 <= s - LAG_R < NG - 1:
                 recip(s - LAG_R)
-                if SIZES[s - LAG_R] == 2:
+                if 2 <= s - LAG_R < NG - 2:
                     gnorm(s - LAG_R)
             if s < NG:
                 copy_out(s, True)

@@ -22,12 +22,12 @@ NPAIR = B * J // 2
 PPB = J // 2
 SIZES = [1, 1] + [2] * 15
 NG = 17
-VCOPY = [2, 3, 4, 5]
-LAG_Q, LAG_X, LAG_E, LAG_R, LAG_N = 1, 2, 3, 4, 5
-GUNITS = 2
+VCOPY = [3, 4, 5, 7, 9, 11, 13, 15]
+LAG_Q, LAG_X, LAG_E, LAG_R, LAG_N = 1, 2, 3, 4, 4
+GT_PLAIN, GT_COPY = 2, 3
+GLAST = 2
 VSPLIT = 1280
 VFIRST = 1
-LAST_ON_SCALAR = 4
 
 
 def tile_multiheadattention_pb_t_kernel(tc, Q, WQ, out_0, out_1):
@@ -58,7 +58,7 @@ def tile_multiheadattention_pb_t_kernel(tc, Q, WQ, out_0, out_1):
         wgrp = const.tile([P, H * DK, 4], BF16, name="wgrp", align_bytes=64)
         wcodes = const.tile([P, H * DK], U32, name="wcodes", align_bytes=64)
         wscl = const.tile([P, H * DK], U8, name="wscl", align_bytes=64)
-        o0 = [[keep.tile([P, J * DK], F32, name="o0_%d_%d" % (b, h)) for h in range(H)] for b in range(B)]
+        o0 = [keep.tile([P, H, J * DK], F32, name="o0_%d" % b) for b in range(B)]
         f8 = [[keep.tile([P, J * DK], FP8, name="f8_%d_%d" % (b, h)) for h in range(H)] for b in range(B)]
 
         nc.vector.memset(zero[:], 0.0)
@@ -70,8 +70,11 @@ def tile_multiheadattention_pb_t_kernel(tc, Q, WQ, out_0, out_1):
         def pairs(g):
             return range(FIRST[g], FIRST[g] + SIZES[g])
 
+        def place(g):
+            return FIRST[g] // PPB, 2 * (FIRST[g] % PPB)
+
         def load(g):
-            b, j0 = FIRST[g] // PPB, 2 * (FIRST[g] % PPB)
+            b, j0 = place(g)
             t = raw.tile([P, 2 * SIZES[g], D], BF16, name="qraw", tag="qraw")
             qraw[g] = t
             nc.sync.dma_start(out=t[:], in_=q_view[b, :, j0:j0 + 2 * SIZES[g], :])
@@ -142,29 +145,32 @@ def tile_multiheadattention_pb_t_kernel(tc, Q, WQ, out_0, out_1):
             rss[g] = rs
             nc.vector.reciprocal(out=rs[:], in_=sums[:, 4 * FIRST[g]:4 * (FIRST[g] + SIZES[g])])
 
-        def gnorm(g):
-            b, j0 = FIRST[g] // PPB, 2 * (FIRST[g] % PPB)
-            nc.gpsimd.tensor_tensor(out=o0[b][1][:, j0 * DK:(j0 + GUNITS) * DK].rearrange("p (t d) -> p t d", d=DK),
-                                    in0=gts[g][:, 1:2 * GUNITS:2, :],
-                                    in1=rss[g][:, 1:2 * GUNITS:2].unsqueeze(2).to_broadcast([P, GUNITS, DK]), op=ALU.mult)
+        def gshare(g):
+            if not 2 <= g < NG - GLAST:
+                return 0
+            return GT_COPY if g + LAG_R in VCOPY else GT_PLAIN
 
-        def norm(g, on_scalar, skip):
-            b, j0 = FIRST[g] // PPB, 2 * (FIRST[g] % PPB)
-            rs = rss[g]
-            n = 0
-            for h in range(H):
-                for t in range(2 * SIZES[g]):
-                    c = 2 * t + h
-                    dst = o0[b][h][:, (j0 + t) * DK:(j0 + t + 1) * DK]
-                    n += 1
-                    if h == 1 and t < skip:
-                        continue
-                    if n > 4 * SIZES[g] - on_scalar:
-                        nc.scalar.activation(out=dst, in_=gts[g][:, c, :], func=ACT.Copy, scale=rs[:, c:c + 1])
-                    else:
-                        nc.vector.tensor_scalar(out=dst, in0=gts[g][:, c, :], scalar1=rs[:, c:c + 1], scalar2=None, op0=ALU.mult)
-                cols = slice(j0 * DK, (j0 + 2 * SIZES[g]) * DK)
-                nc.sync.dma_start(out=o0_view[b, h, :, cols], in_=o0[b][h][:, cols])
+        def gnorm(g):
+            b, j0 = place(g)
+            n = gshare(g)
+            if n == 0:
+                return
+            nc.gpsimd.tensor_tensor(out=o0[b][:, :, j0 * DK:(j0 + n) * DK].rearrange("p h (t d) -> p h t d", d=DK),
+                                    in0=gts[g][:, 0:2 * n, :].rearrange("p (t h) d -> p h t d", h=H),
+                                    in1=rss[g][:, 0:2 * n].rearrange("p (t h) -> p h t", h=H).unsqueeze(3).to_broadcast([P, H, n, DK]),
+                                    op=ALU.mult)
+
+        def norm(g, h, on_scalar):
+            b, j0 = place(g)
+            for t in range(gshare(g), 2 * SIZES[g]):
+                c = 2 * t + h
+                dst = o0[b][:, h, (j0 + t) * DK:(j0 + t + 1) * DK]
+                if on_scalar:
+                    nc.scalar.activation(out=dst, in_=gts[g][:, c, :], func=ACT.Copy, scale=rss[g][:, c:c + 1])
+                else:
+                    nc.vector.tensor_scalar(out=dst, in0=gts[g][:, c, :], scalar1=rss[g][:, c:c + 1], scalar2=None, op0=ALU.mult)
+            cols = slice(j0 * DK, (j0 + 2 * SIZES[g]) * DK)
+            nc.sync.dma_start(out=o0_view[b, h, :, cols], in_=o0[b][:, h, cols])
 
         load(0)
         nc.sync.dma_start(out=wraw[:], in_=w_view)
@@ -179,7 +185,7 @@ def tile_multiheadattention_pb_t_kernel(tc, Q, WQ, out_0, out_1):
                 nc.tensor.transpose(out=wt[:, u, h * P:(h + 1) * P], in_=wwords[:, u:D // 2:2], identity=ident[:])
         nc.vector.tensor_copy(out=wgrp[:].bitcast(F32), in_=wt[:].rearrange("p u r -> p r u"))
 
-        for s in range(NG + LAG_N - 1):
+        for s in range(NG + LAG_X):
             if 0 <= s - LAG_X < NG:
                 mult(s - LAG_X)
             if s + 1 < NG:
@@ -188,29 +194,34 @@ def tile_multiheadattention_pb_t_kernel(tc, Q, WQ, out_0, out_1):
                 copy_out(s, False)
             if 0 <= s - LAG_E < NG:
                 expo(s - LAG_E)
+            if 0 <= s - LAG_R:
+                recip(s - LAG_R)
+                gnorm(s - LAG_R)
             if s == 1:
                 nc.vector.quantize_mx(out=wcodes[:].bitcast(FP8X4), scales=wscl[:],
                                       in_=wgrp[:].rearrange("p r t -> p (r t)"))
             if 0 <= s - LAG_Q < NG:
                 quant(s - LAG_Q)
-            if 0 <= s - LAG_N:
-                norm(s - LAG_N, 0, GUNITS if 2 <= s - LAG_N < NG - 2 else 0)
-            if 0 <= s - LAG_R < NG - 1:
-                recip(s - LAG_R)
-                if 2 <= s - LAG_R < NG - 2:
-                    gnorm(s - LAG_R)
             if s < NG:
                 copy_out(s, True)
             if 0 <= s - LAG_X < NG:
                 rowmax(s - LAG_X)
-            if s == NG + LAG_E - 1:
-                nc.vector.tensor_reduce(out=sums[:, 4 * NPAIR:4 * NPAIR + 1], in_=sums[:, 0:4 * FIRST[NG - 1]], axis=AX.X, op=ALU.min)
+            if 0 <= s - LAG_N:
+                norm(s - LAG_N, 0, False)
+                norm(s - LAG_N, 1, False)
+
+        expo(NG - 1)
+        recip(NG - 2)
+        nc.vector.tensor_reduce(out=sums[:, 4 * NPAIR:4 * NPAIR + 1], in_=sums[:, 0:4 * FIRST[NG - 1]], axis=AX.X, op=ALU.min)
+        norm(NG - 2, 0, False)
+        norm(NG - 2, 1, True)
 
         nc.vector.tensor_reduce(out=pmin[:], in_=sums[:, 4 * FIRST[NG - 1]:4 * NPAIR + 1], axis=AX.X, op=ALU.min)
         at = tps.tile([P, 2, 2 * P], F32, name="xt", tag="xt")
         nc.tensor.transpose(out=at[:, 0, 0:P], in_=pmin[:, 0:1].to_broadcast([P, P]), identity=ident[:])
         recip(NG - 1)
-        norm(NG - 1, LAST_ON_SCALAR, 0)
+        norm(NG - 1, 0, False)
+        norm(NG - 1, 1, True)
         nc.vector.tensor_scalar(out=scaled[:], in0=at[:, 0, 0:P], scalar1=448.0, scalar2=None, op0=ALU.mult, op1=ALU.min,
                                 accum_out=rfac[:, 0:1])
 
@@ -219,10 +230,10 @@ def tile_multiheadattention_pb_t_kernel(tc, Q, WQ, out_0, out_1):
             for h in range(H):
                 vs = J * DK if n < VFIRST else VSPLIT
                 n += 1
-                nc.vector.tensor_scalar(out=f8[b][h][:, 0:vs], in0=o0[b][h][:, 0:vs], scalar1=rfac[:, 0:1],
+                nc.vector.tensor_scalar(out=f8[b][h][:, 0:vs], in0=o0[b][:, h, 0:vs], scalar1=rfac[:, 0:1],
                                         scalar2=None, op0=ALU.mult, saturate=False)
                 if vs < J * DK:
-                    nc.scalar.activation(out=f8[b][h][:, vs:J * DK], in_=o0[b][h][:, vs:J * DK], func=ACT.Identity,
+                    nc.scalar.activation(out=f8[b][h][:, vs:J * DK], in_=o0[b][:, h, vs:J * DK], func=ACT.Identity,
                                          scale=rfac[:, 0:1], bias=zero[:, 0:1], saturate=False)
                 if n < B * H:
                     nc.sync.dma_start(out=o1_view[b, h], in_=f8[b][h][:].bitcast(U8))

@@ -22,9 +22,9 @@ NPAIR = B * J // 2
 PPB = J // 2
 SIZES = [1, 1] + [2] * 15
 NG = 17
-VCOPY = [3, 4, 5, 7, 9, 11, 13, 15]
+VCOPY = [2, 3, 4, 5, 9, 13]
 LAG_Q, LAG_X, LAG_E, LAG_R, LAG_N = 1, 2, 3, 4, 4
-GT_PLAIN, GT_COPY = 2, 3
+GT_PLAIN, GT_COPY = 3, 4
 GLAST = 2
 VSPLIT = 1280
 VFIRST = 1
@@ -155,14 +155,13 @@ def tile_multiheadattention_pb_t_kernel(tc, Q, WQ, out_0, out_1):
             n = gshare(g)
             if n == 0:
                 return
-            nc.gpsimd.tensor_tensor(out=o0[b][:, :, j0 * DK:(j0 + n) * DK].rearrange("p h (t d) -> p h t d", d=DK),
-                                    in0=gts[g][:, 0:2 * n, :].rearrange("p (t h) d -> p h t d", h=H),
-                                    in1=rss[g][:, 0:2 * n].rearrange("p (t h) -> p h t", h=H).unsqueeze(3).to_broadcast([P, H, n, DK]),
-                                    op=ALU.mult)
+            nc.gpsimd.tensor_tensor(out=o0[b][:, 1, j0 * DK:(j0 + n) * DK].rearrange("p (t d) -> p t d", d=DK),
+                                    in0=gts[g][:, 1:2 * n:2, :],
+                                    in1=rss[g][:, 1:2 * n:2].unsqueeze(2).to_broadcast([P, n, DK]), op=ALU.mult)
 
         def norm(g, h, on_scalar):
             b, j0 = place(g)
-            for t in range(gshare(g), 2 * SIZES[g]):
+            for t in range(gshare(g) if h == 1 else 0, 2 * SIZES[g]):
                 c = 2 * t + h
                 dst = o0[b][:, h, (j0 + t) * DK:(j0 + t + 1) * DK]
                 if on_scalar:

@@ -28,6 +28,8 @@ GT_PLAIN, GT_COPY = 3, 4
 GLAST = 2
 VSPLIT = 1280
 VFIRST = 1
+LASTP = 2
+NFINE = 4
 
 
 def tile_multiheadattention_pb_t_kernel(tc, Q, WQ, out_0, out_1):
@@ -77,7 +79,9 @@ def tile_multiheadattention_pb_t_kernel(tc, Q, WQ, out_0, out_1):
             b, j0 = place(g)
             t = raw.tile([P, 2 * SIZES[g], D], BF16, name="qraw", tag="qraw")
             qraw[g] = t
-            nc.sync.dma_start(out=t[:], in_=q_view[b, :, j0:j0 + 2 * SIZES[g], :])
+            step = 2 if g < NFINE else 2 * SIZES[g]
+            for a in range(0, 2 * SIZES[g], step):
+                nc.sync.dma_start(out=t[:, a:a + step, :], in_=q_view[b, :, j0 + a:j0 + a + step, :])
 
         def turn(g):
             for q in pairs(g):
@@ -229,13 +233,17 @@ def tile_multiheadattention_pb_t_kernel(tc, Q, WQ, out_0, out_1):
             for h in range(H):
                 vs = J * DK if n < VFIRST else VSPLIT
                 n += 1
-                nc.vector.tensor_scalar(out=f8[b][h][:, 0:vs], in0=o0[b][:, h, 0:vs], scalar1=rfac[:, 0:1],
-                                        scalar2=None, op0=ALU.mult, saturate=False)
-                if vs < J * DK:
-                    nc.scalar.activation(out=f8[b][h][:, vs:J * DK], in_=o0[b][:, h, vs:J * DK], func=ACT.Identity,
-                                         scale=rfac[:, 0:1], bias=zero[:, 0:1], saturate=False)
+                parts = LASTP if n == B * H else 1
+                vw, sw = vs // parts, (J * DK - vs) // parts
+                for i in range(parts):
+                    v0, s0 = i * vw, vs + i * sw
+                    nc.vector.tensor_scalar(out=f8[b][h][:, v0:v0 + vw], in0=o0[b][:, h, v0:v0 + vw], scalar1=rfac[:, 0:1],
+                                            scalar2=None, op0=ALU.mult, saturate=False)
+                    if sw > 0:
+                        nc.scalar.activation(out=f8[b][h][:, s0:s0 + sw], in_=o0[b][:, h, s0:s0 + sw], func=ACT.Identity,
+                                             scale=rfac[:, 0:1], bias=zero[:, 0:1], saturate=False)
+                    if n == B * H:
+                        nc.sync.dma_start(out=o1_view[b, h, :, v0:v0 + vw], in_=f8[b][h][:, v0:v0 + vw].bitcast(U8))
+                        nc.sync.dma_start(out=o1_view[b, h, :, s0:s0 + sw], in_=f8[b][h][:, s0:s0 + sw].bitcast(U8))
                 if n < B * H:
                     nc.sync.dma_start(out=o1_view[b, h], in_=f8[b][h][:].bitcast(U8))
-                else:
-                    nc.sync.dma_start(out=o1_view[b, h, :, 0:vs], in_=f8[b][h][:, 0:vs].bitcast(U8))
-                    nc.sync.dma_start(out=o1_view[b, h, :, vs:J * DK], in_=f8[b][h][:, vs:J * DK].bitcast(U8))

@@ -28,6 +28,7 @@ GT_PLAIN, GT_COPY = 3, 4
 GLAST = 2
 VSPLIT = 1280
 VFIRST = 1
+NWARM = 4
 LASTP = 2
 NFINE = 4
 
@@ -174,6 +175,10 @@ def tile_multiheadattention_pb_t_kernel(tc, Q, WQ, out_0, out_1):
                     nc.vector.tensor_scalar(out=dst, in0=gts[g][:, c, :], scalar1=rss[g][:, c:c + 1], scalar2=None, op0=ALU.mult)
             cols = slice(j0 * DK, (j0 + 2 * SIZES[g]) * DK)
             nc.sync.dma_start(out=o0_view[b, h, :, cols], in_=o0[b][:, h, cols])
+
+        wm = tps.tile([P, 2, 2 * P], F32, name="xt", tag="xt")
+        for i in range(NWARM):
+            nc.tensor.matmul(out=wm[:, 0, 0:P], lhsT=ident[:], rhs=ident[:], start=True, stop=True)
 
         load(0)
         nc.sync.dma_start(out=wraw[:], in_=w_view)

@@ -38,7 +38,7 @@ def tile_multiheadattention_pb_t_kernel(tc, Q, WQ, out_0, out_1):
     FIRST = [sum(SIZES[:g]) for g in range(NG)]
     q_view = Q.rearrange("b (p j) k -> b p j k", j=J)
     w_view = WQ.rearrange("(h p) k -> p h k", p=P)
-    o0_view = out_0.rearrange("b h (p j) d -> b h p (j d)", j=J)
+    o0_view = out_0.rearrange("b h (p j) d -> b p h (j d)", j=J)
     o1_view = out_1.rearrange("b h (p j) d -> b h p (j d)", j=J)
 
     with ExitStack() as ctx:
@@ -173,8 +173,9 @@ def tile_multiheadattention_pb_t_kernel(tc, Q, WQ, out_0, out_1):
                     nc.scalar.activation(out=dst, in_=gts[g][:, c, :], func=ACT.Copy, scale=rss[g][:, c:c + 1])
                 else:
                     nc.vector.tensor_scalar(out=dst, in0=gts[g][:, c, :], scalar1=rss[g][:, c:c + 1], scalar2=None, op0=ALU.mult)
-            cols = slice(j0 * DK, (j0 + 2 * SIZES[g]) * DK)
-            nc.sync.dma_start(out=o0_view[b, h, :, cols], in_=o0[b][:, h, cols])
+            if h == H - 1:
+                cols = slice(j0 * DK, (j0 + 2 * SIZES[g]) * DK)
+                nc.sync.dma_start(out=o0_view[b, :, :, cols], in_=o0[b][:, :, cols])
 
         wm = tps.tile([P, 2, 2 * P], F32, name="xt", tag="xt")
         for i in range(NWARM):

@@ -225,6 +225,10 @@ def tile_multiheadattention_pb_t_kernel(tc, Q, WQ, out_0, out_1):
         norm(NG - 2, 0, False)
         norm(NG - 2, 1, True)
 
+        wm2 = tps.tile([P, 2, 2 * P], F32, name="xt", tag="xt")
+        for g, c in [(NG - 2, 1), (NG - 2, 3), (NG - 2, 5), (NG - 2, 7), (NG - 1, 1), (NG - 1, 3), (NG - 1, 5)]:
+            nc.tensor.matmul(out=wm2[:, 0, 0:P], lhsT=ident[:], rhs=gts[g][:, c, :], start=True, stop=True)
+
         nc.vector.tensor_reduce(out=pmin[:], in_=sums[:, 4 * FIRST[NG - 1]:4 * NPAIR + 1], axis=AX.X, op=ALU.min)
         at = tps.tile([P, 2, 2 * P], F32, name="xt", tag="xt")
         nc.tensor.transpose(out=at[:, 0, 0:P], in_=pmin[:, 0:1].to_broadcast([P, P]), identity=ident[:])

from contextlib import ExitStack

import concourse.mybir as mybir
from concourse.masks import make_identity

B, N, D, H, DK = 4, 2048, 512, 2, 128
FLOPS = 2 * B * N * D * H * DK

F32 = mybir.dt.float32
BF16 = mybir.dt.bfloat16
U32 = mybir.dt.uint32
U8 = mybir.dt.uint8
FP8X4 = mybir.dt.float8_e4m3fn_x4
FP8 = mybir.dt.float8_e4m3fn
ACT = mybir.ActivationFunctionType
ALU = mybir.AluOpType
AX = mybir.AxisListType

P = 128
J = N // P
NPAIR = B * J // 2
PPB = J // 2
SIZES = [1, 1] + [2] * 15
NG = 17
VCOPY = [2, 3, 4, 5, 9, 13]
LAG_Q, LAG_X, LAG_E, LAG_R, LAG_N = 1, 2, 3, 4, 4
GT_PLAIN, GT_COPY = 3, 4
GLAST = 2
VSPLIT = 1280
VFIRST = 1
NWARM = 4
LASTP = 2
NFINE = 4


def tile_multiheadattention_pb_t_kernel(tc, Q, WQ, out_0, out_1):
    nc = tc.nc
    FIRST = [sum(SIZES[:g]) for g in range(NG)]
    q_view = Q.rearrange("b (p j) k -> b p j k", j=J)
    w_view = WQ.rearrange("(h p) k -> p h k", p=P)
    o0_view = out_0.rearrange("b h (p j) d -> b p h (j d)", j=J)
    o1_view = out_1.rearrange("b h (p j) d -> b h p (j d)", j=J)

    with ExitStack() as ctx:
        ctx.enter_context(tc.manual_schedule())
        const = ctx.enter_context(tc.tile_pool(name="const", bufs=1))
        raw = ctx.enter_context(tc.tile_pool(name="raw", bufs=NG))
        work = ctx.enter_context(tc.tile_pool(name="work", bufs=5))
        keep = ctx.enter_context(tc.tile_pool(name="keep", bufs=1))
        tps = ctx.enter_context(tc.psum_pool(name="tps", bufs=4))
        qps = ctx.enter_context(tc.psum_pool(name="qps", bufs=4))

        zero = const.tile([P, 1], F32, name="zero")
        warm = const.tile([P, 1], F32, name="warm")
        ident = const.tile([P, P], F32, name="ident")
        sums = const.tile([P, 4 * NPAIR + 1], F32, name="sums")
        pmin = const.tile([P, 1], F32, name="pmin")
        scaled = const.tile([P, P], F32, name="scaled")
        rfac = const.tile([P, 1], F32, name="rfac")
        wraw = const.tile([P, H, D], BF16, name="wraw")
        wgrp = const.tile([P, H * DK, 4], BF16, name="wgrp", align_bytes=64)
        wcodes = const.tile([P, H * DK], U32, name="wcodes", align_bytes=64)
        wscl = const.tile([P, H * DK], U8, name="wscl", align_bytes=64)
        o0 = [keep.tile([P, H, J * DK], F32, name="o0_%d" % b) for b in range(B)]
        f8 = [[keep.tile([P, J * DK], FP8, name="f8_%d_%d" % (b, h)) for h in range(H)] for b in range(B)]

        nc.vector.memset(zero[:], 0.0)
        nc.scalar.activation(out=warm[:], in_=zero[:], func=ACT.Exp)
        make_identity(nc, ident[:])

        qraw, xts, grps, cods, scls, qbs, nms, gts, rss = {}, {}, {}, {}, {}, {}, {}, {}, {}

        def pairs(g):
            return range(FIRST[g], FIRST[g] + SIZES[g])

        def place(g):
            return FIRST[g] // PPB, 2 * (FIRST[g] % PPB)

        def load(g):
            b, j0 = place(g)
            t = raw.tile([P, 2 * SIZES[g], D], BF16, name="qraw", tag="qraw")
            qraw[g] = t
            step = 2 if g < NFINE else 2 * SIZES[g]
            for a in range(0, 2 * SIZES[g], step):
                nc.sync.dma_start(out=t[:, a:a + step, :], in_=q_view[b, :, j0 + a:j0 + a + step, :])

        def turn(g):
            for q in pairs(g):
                xt = tps.tile([P, 2, 2 * P], F32, name="xt", tag="xt")
                xts[q] = xt
                for a in range(2):
                    words = qraw[g][:, 2 * (q - FIRST[g]) + a, :].bitcast(F32)
                    for u in range(2):
                        nc.tensor.transpose(out=xt[:, u, a * P:(a + 1) * P], in_=words[:, u:D // 2:2], identity=ident[:])

        def copy_out(g, on_vector):
            if g not in grps:
                grps[g] = work.tile([P, SIZES[g] * 2 * P, 4], BF16, name="grp", tag="grp", align_bytes=64)
            for q in pairs(g):
                v = g in VCOPY and q == FIRST[g] + SIZES[g] - 1
                if v != on_vector:
                    continue
                l = q - FIRST[g]
                dst = grps[g][:, l * 2 * P:(l + 1) * 2 * P, :].bitcast(F32)
                src = xts[q][:].rearrange("p u r -> p r u")
                if on_vector:
                    nc.vector.tensor_copy(out=dst, in_=src)
                else:
                    nc.scalar.copy(out=dst, in_=src)

        def quant(g):
            cod = work.tile([P, SIZES[g] * 2 * P], U32, name="cod", tag="cod", align_bytes=64)
            scl = work.tile([P, SIZES[g] * 2 * P], U8, name="scl", tag="scl", align_bytes=64)
            cods[g], scls[g] = cod, scl
            nc.vector.quantize_mx(out=cod[:].bitcast(FP8X4), scales=scl[:],
                                  in_=grps[g][:].rearrange("p r t -> p (r t)"))

        def mult(g):
            for q in pairs(g):
                qb = qps.tile([P, 2, H * DK], F32, name="qb", tag="qb")
                qbs[q] = qb
                for a in range(2):
                    c0 = (2 * (q - FIRST[g]) + a) * P
                    nc.tensor.matmul_mx(out=qb[:, a, :], lhsT=cods[g][:, c0:c0 + P].bitcast(FP8X4), lhsT_scale=scls[g][:, c0:c0 + P],
                                        rhs=wcodes[:].bitcast(FP8X4), rhs_scale=wscl[:], start=True, stop=True)

        def rowmax(g):
            nm = work.tile([P, 4 * SIZES[g]], F32, name="nm", tag="nm")
            nms[g] = nm
            for q in pairs(g):
                l = q - FIRST[g]
                nc.vector.tensor_reduce(out=nm[:, 4 * l:4 * l + 4],
                                        in_=qbs[q][:].rearrange("p a (h d) -> p (a h) d", h=H),
                                        axis=AX.X, op=ALU.max, negate=True)

        def expo(g):
            gt = work.tile([P, 4 * SIZES[g], DK], F32, name="gt", tag="gt")
            gts[g] = gt
            for q in pairs(g):
                l = q - FIRST[g]
                for a in range(2):
                    for h in range(H):
                        c = 4 * l + 2 * a + h
                        nc.scalar.activation(out=gt[:, c, :], in_=qbs[q][:, a, h * DK:(h + 1) * DK], func=ACT.Exp,
                                             bias=nms[g][:, c:c + 1], scale=1.0,
                                             accum_out=sums[:, 4 * FIRST[g] + c:4 * FIRST[g] + c + 1])

        def recip(g):
            rs = work.tile([P, 4 * SIZES[g]], F32, name="rs", tag="rs")
            rss[g] = rs
            nc.vector.reciprocal(out=rs[:], in_=sums[:, 4 * FIRST[g]:4 * (FIRST[g] + SIZES[g])])

        def gshare(g):
            if not 2 <= g < NG - GLAST:
                return 0
            return GT_COPY if g + LAG_R in VCOPY else GT_PLAIN

        def gnorm(g):
            b, j0 = place(g)
            n = gshare(g)
            if n == 0:
                return
            nc.gpsimd.tensor_tensor(out=o0[b][:, 1, j0 * DK:(j0 + n) * DK].rearrange("p (t d) -> p t d", d=DK),
                                    in0=gts[g][:, 1:2 * n:2, :],
                                    in1=rss[g][:, 1:2 * n:2].unsqueeze(2).to_broadcast([P, n, DK]), op=ALU.mult)

        def norm(g, h, on_scalar):
            b, j0 = place(g)
            for t in range(gshare(g) if h == 1 else 0, 2 * SIZES[g]):
                c = 2 * t + h
                dst = o0[b][:, h, (j0 + t) * DK:(j0 + t + 1) * DK]
                if on_scalar:
                    nc.scalar.activation(out=dst, in_=gts[g][:, c, :], func=ACT.Copy, scale=rss[g][:, c:c + 1])
                else:
                    nc.vector.tensor_scalar(out=dst, in0=gts[g][:, c, :], scalar1=rss[g][:, c:c + 1], scalar2=None, op0=ALU.mult)
            if h == H - 1:
                cols = slice(j0 * DK, (j0 + 2 * SIZES[g]) * DK)
                nc.sync.dma_start(out=o0_view[b, :, :, cols], in_=o0[b][:, :, cols])

        wm = tps.tile([P, 2, 2 * P], F32, name="xt", tag="xt")
        for i in range(NWARM):
            nc.tensor.matmul(out=wm[:, 0, 0:P], lhsT=ident[:], rhs=ident[:], start=True, stop=True)

        load(0)
        nc.sync.dma_start(out=wraw[:], in_=w_view)
        for g in range(1, NG):
            load(g)

        turn(0)
        wt = tps.tile([P, 2, 2 * P], F32, name="xt", tag="xt")
        for h in range(H):
            wwords = wraw[:, h, :].bitcast(F32)
            for u in range(2):
                nc.tensor.transpose(out=wt[:, u, h * P:(h + 1) * P], in_=wwords[:, u:D // 2:2], identity=ident[:])
        nc.vector.tensor_copy(out=wgrp[:].bitcast(F32), in_=wt[:].rearrange("p u r -> p r u"))

        for s in range(NG + LAG_X):
            if 0 <= s - LAG_X < NG:
                mult(s - LAG_X)
            if s + 1 < NG:
                turn(s + 1)
            if s < NG:
                copy_out(s, False)
            if 0 <= s - LAG_E < NG:
                expo(s - LAG_E)
            if 0 <= s - LAG_R:
                recip(s - LAG_R)
                gnorm(s - LAG_R)
            if s == 1:
                nc.vector.quantize_mx(out=wcodes[:].bitcast(FP8X4), scales=wscl[:],
                                      in_=wgrp[:].rearrange("p r t -> p (r t)"))
            if 0 <= s - LAG_Q < NG:
                quant(s - LAG_Q)
            if s < NG:
                copy_out(s, True)
            if 0 <= s - LAG_X < NG:
                rowmax(s - LAG_X)
            if 0 <= s - LAG_N:
                norm(s - LAG_N, 0, False)
                norm(s - LAG_N, 1, False)

        expo(NG - 1)
        recip(NG - 2)
        nc.vector.tensor_reduce(out=sums[:, 4 * NPAIR:4 * NPAIR + 1], in_=sums[:, 0:4 * FIRST[NG - 1]], axis=AX.X, op=ALU.min)
        norm(NG - 2, 0, False)
        norm(NG - 2, 1, True)

        wm2 = tps.tile([P, 2, 2 * P], F32, name="xt", tag="xt")
        for g, c in [(NG - 2, 1), (NG - 2, 3), (NG - 2, 5), (NG - 2, 7), (NG - 1, 1), (NG - 1, 3), (NG - 1, 5)]:
            nc.tensor.matmul(out=wm2[:, 0, 0:P], lhsT=ident[:], rhs=gts[g][:, c, :], start=True, stop=True)

        nc.vector.tensor_reduce(out=pmin[:], in_=sums[:, 4 * FIRST[NG - 1]:4 * NPAIR + 1], axis=AX.X, op=ALU.min)
        at = tps.tile([P, 2, 2 * P], F32, name="xt", tag="xt")
        nc.tensor.transpose(out=at[:, 0, 0:P], in_=pmin[:, 0:1].to_broadcast([P, P]), identity=ident[:])
        recip(NG - 1)
        norm(NG - 1, 0, False)
        norm(NG - 1, 1, True)
        nc.vector.tensor_scalar(out=scaled[:], in0=at[:, 0, 0:P], scalar1=448.0, scalar2=None, op0=ALU.mult, op1=ALU.min,
                                accum_out=rfac[:, 0:1])

        n = 0
        for b in range(B):
            for h in range(H):
                vs = J * DK if n < VFIRST else VSPLIT
                n += 1
                parts = LASTP if n == B * H else 1
                vw, sw = vs // parts, (J * DK - vs) // parts
                for i in range(parts):
                    v0, s0 = i * vw, vs + i * sw
                    nc.vector.tensor_scalar(out=f8[b][h][:, v0:v0 + vw], in0=o0[b][:, h, v0:v0 + vw], scalar1=rfac[:, 0:1],
                                            scalar2=None, op0=ALU.mult, saturate=False)
                    if sw > 0:
                        nc.scalar.activation(out=f8[b][h][:, s0:s0 + sw], in_=o0[b][:, h, s0:s0 + sw], func=ACT.Identity,
                                             scale=rfac[:, 0:1], bias=zero[:, 0:1], saturate=False)
                    if n == B * H:
                        nc.sync.dma_start(out=o1_view[b, h, :, v0:v0 + vw], in_=f8[b][h][:, v0:v0 + vw].bitcast(U8))
                        nc.sync.dma_start(out=o1_view[b, h, :, s0:s0 + sw], in_=f8[b][h][:, s0:s0 + sw].bitcast(U8))
                if n < B * H:
                    nc.sync.dma_start(out=o1_view[b, h], in_=f8[b][h][:].bitcast(U8))
